import numpy as np
import ml_dtypes


def mxq(x, axis, fmt="e4m3"):
    dtype, down = {"e4m3": (ml_dtypes.float8_e4m3fn, 7), "e5m2": (ml_dtypes.float8_e5m2, 14)}[fmt]
    v = np.moveaxis(np.asarray(x, np.float32).astype(ml_dtypes.bfloat16).astype(np.float64), axis, -1)
    blocks = v.reshape(v.shape[:-1] + (-1, 32))
    amax = np.abs(blocks).max(-1, keepdims=True)
    byte = np.maximum(np.where(amax > 0, np.frexp(amax)[1] - 1 + 127, 0) - down, 1)
    scale = np.exp2(byte - 127.0)
    codes = (blocks / scale).astype(np.float32).astype(dtype).astype(np.float64)
    return np.moveaxis((codes * scale).reshape(v.shape), -1, axis)


WIDE = False


def mx_kscale(k):
    if not WIDE:
        return np.ones(k)
    levels = np.array([10, -10, 5, -5, 0])
    a = np.random.permutation(np.resize(levels, k // 512 * 4)).reshape(k // 512, 4)
    idx = np.arange(k)
    return np.exp2(a[idx // 512, idx % 128 // 32])


BF16 = ml_dtypes.bfloat16


def bf(x):
    return np.asarray(x, np.float32).astype(BF16)


def f64(x):
    return np.asarray(x).astype(np.float64)


B, N, L, H, S, R, C = 2, 512, 4, 16, 2, 2, 512


def setup_inputs():
    s = mx_kscale(N)
    return {"x": bf(np.random.standard_normal((B, N, L, H)) * s[None, :, None, None]),
            "support": bf(np.random.standard_normal((S, N, N)) * 0.6 / np.sqrt(N) * s[:, None] / s[None, :]),
            "eps": bf(np.random.uniform(0.1, 0.3, (1,)))}


def reference(x, support, eps):
    xv = f64(x).reshape(B, N, L * H)
    sup = f64(support)
    g = 1.0 + f64(eps)
    xq = mxq(xv, 1, "e4m3")
    res = []
    for i in range(S):
        aq = mxq(sup[i], 1, "e4m3")
        out, oq = xv, xq
        for j in range(R):
            out = g * out + (aq @ oq)
            res.append(out)
            if j + 1 < R:
                oq = mxq(out, 1, "e4m3")
    return np.stack(res, axis=-1).reshape(B, N, L, H * len(res))

@@ -1,0 +1,158 @@
+from contextlib import ExitStack
+
+import concourse.mybir as mybir
+from concourse.masks import make_identity
+
+F32 = mybir.dt.float32
+BF16 = mybir.dt.bfloat16
+U32 = mybir.dt.uint32
+U8 = mybir.dt.uint8
+FP8X4 = mybir.dt.float8_e4m3fn_x4
+MULT = mybir.AluOpType.mult
+ADD = mybir.AluOpType.add
+
+P = 128
+PACK = 4
+BATCH = 2
+NODES = P * PACK
+FEAT = 64
+COLS = BATCH * FEAT
+SUPPORTS = 2
+HOPS = 2
+RESULTS = SUPPORTS * HOPS
+HALF = PACK // 2
+
+FLOPS = 2 * RESULTS * NODES * NODES * COLS
+
+
+def tile_ginconvfft_pa_s_kernel(tc, x, support, eps, out):
+    nc = tc.nc
+    with ExitStack() as ctx:
+        keep = ctx.enter_context(tc.tile_pool(name="keep", bufs=1))
+        psum = ctx.enter_context(tc.psum_pool(name="psum", bufs=1))
+
+        a_rows = {}
+        for i in range(SUPPORTS):
+            by_class = support[i].rearrange("(p c) m -> p c m", c=PACK)
+            for half in range(2):
+                classes = slice(half * HALF, (half + 1) * HALF)
+                a_rows[i, half] = keep.tile([P, HALF, NODES], BF16, name="a_rows_%d_%d" % (i, half))
+                nc.sync.dma_start(out=a_rows[i, half][:], in_=by_class[:, classes, :])
+        x_rows = keep.tile([P, BATCH, PACK, FEAT], BF16)
+        nc.scalar.dma_start(out=x_rows[:], in_=x.rearrange("b (p c) l h -> p b c (l h)", c=PACK))
+        eps_col = keep.tile([P, 1], BF16)
+        nc.scalar.dma_start(out=eps_col[:], in_=eps.partition_broadcast(P))
+
+        identity = keep.tile([P, P], F32)
+        make_identity(nc, identity[:])
+
+        x_grouped = keep.tile([P, COLS, PACK], BF16, align_bytes=64)
+        nc.vector.tensor_copy(
+            out=x_grouped[:].rearrange("p (b f) c -> p b f c", b=BATCH),
+            in_=x_rows[:].rearrange("p b c f -> p b f c"),
+        )
+        x_codes = keep.tile([P, COLS], U32, align_bytes=64)
+        x_scales = keep.tile([P, COLS], U8, align_bytes=64)
+        nc.vector.quantize_mx(
+            out=x_codes[:].bitcast(FP8X4),
+            scales=x_scales[:],
+            in_=x_grouped[:].rearrange("p w c -> p (w c)"),
+        )
+        gain = keep.tile([P, 1], F32)
+        nc.vector.tensor_scalar_add(out=gain[:], in0=eps_col[:], scalar1=1.0)
+
+        a_codes = {}
+        a_scales = {}
+        for i in range(SUPPORTS):
+            for half in range(2):
+                words = a_rows[i, half][:].bitcast(F32).rearrange("p c (q u) -> p c q u", u=2)
+                turned = psum.tile([P, HALF, 2, P], F32, name="turned_%d_%d" % (i, half))
+                for c in range(HALF):
+                    for u in range(2):
+                        nc.tensor.transpose(turned[:, c, u, :], words[:, c, :, u], identity[:])
+                a_grouped = keep.tile([P, HALF * P, PACK], BF16, align_bytes=64, name="a_grouped_%d_%d" % (i, half))
+                nc.scalar.copy(
+                    out=a_grouped[:].bitcast(F32).rearrange("q (c r) u -> q c r u", c=HALF),
+                    in_=turned[:].rearrange("q c u r -> q c r u"),
+                )
+                a_codes[i, half] = keep.tile([P, HALF * P], U32, align_bytes=64, name="a_codes_%d_%d" % (i, half))
+                a_scales[i, half] = keep.tile([P, HALF * P], U8, align_bytes=64, name="a_scales_%d_%d" % (i, half))
+                nc.vector.quantize_mx(
+                    out=a_codes[i, half][:].bitcast(FP8X4),
+                    scales=a_scales[i, half][:],
+                    in_=a_grouped[:].rearrange("q w t -> q (w t)"),
+                )
+
+        def hop(i, sums, v_codes, v_scales):
+            for c in range(PACK):
+                half = c // HALF
+                rows = slice((c % HALF) * P, (c % HALF + 1) * P)
+                nc.tensor.matmul_mx(
+                    out=sums[:, c, :],
+                    lhsT=a_codes[i, half][:, rows].bitcast(FP8X4),
+                    lhsT_scale=a_scales[i, half][:, rows],
+                    rhs=v_codes[:].bitcast(FP8X4),
+                    rhs_scale=v_scales[:],
+                    start=True,
+                    stop=True,
+                )
+
+        results = keep.tile([P, RESULTS, PACK, COLS], F32)
+
+        sums1 = {}
+        h1_codes = {}
+        h1_scales = {}
+        for i in range(SUPPORTS):
+            sums1[i] = psum.tile([P, PACK, COLS], F32, name="sums1_%d" % i)
+            hop(i, sums1[i], x_codes, x_scales)
+            h1_grouped = keep.tile([P, COLS, PACK], BF16, align_bytes=64, name="h1_grouped_%d" % i)
+            nc.vector.scalar_tensor_tensor(
+                out=h1_grouped[:],
+                in0=x_grouped[:],
+                scalar=gain[:],
+                in1=sums1[i][:].rearrange("p c w -> p w c"),
+                op0=MULT,
+                op1=ADD,
+            )
+            h1_codes[i] = keep.tile([P, COLS], U32, align_bytes=64, name="h1_codes_%d" % i)
+            h1_scales[i] = keep.tile([P, COLS], U8, align_bytes=64, name="h1_scales_%d" % i)
+            nc.vector.quantize_mx(
+                out=h1_codes[i][:].bitcast(FP8X4),
+                scales=h1_scales[i][:],
+                in_=h1_grouped[:].rearrange("p w c -> p (w c)"),
+            )
+            nc.vector.scalar_tensor_tensor(
+                out=results[:, HOPS * i, :, :],
+                in0=x_grouped[:].rearrange("p w c -> p c w"),
+                scalar=gain[:],
+                in1=sums1[i][:],
+                op0=MULT,
+                op1=ADD,
+            )
+
+        for i in range(SUPPORTS):
+            sums2 = psum.tile([P, PACK, COLS], F32, name="sums2_%d" % i)
+            hop(i, sums2, h1_codes[i], h1_scales[i])
+            nc.vector.scalar_tensor_tensor(
+                out=results[:, HOPS * i + 1, :, :],
+                in0=results[:, HOPS * i, :, :],
+                scalar=gain[:],
+                in1=sums2[:],
+                op0=MULT,
+                op1=ADD,
+            )
+
+        out_by_class = out.rearrange("b (p c) l g -> p b c (l g)", c=PACK)
+        for half in range(2):
+            classes = slice(half * HALF, (half + 1) * HALF)
+            for b in range(BATCH):
+                woven = keep.tile([P, HALF, FEAT, RESULTS], F32, name="woven_%d_%d" % (b, half))
+                source = results[:, :, classes, b * FEAT : (b + 1) * FEAT].rearrange("p k c f -> p c f k")
+                if b == 0:
+                    nc.vector.tensor_copy(out=woven[:], in_=source)
+                else:
+                    nc.scalar.copy(out=woven[:], in_=source)
+                nc.sync.dma_start(
+                    out=out_by_class[:, b, classes, :],
+                    in_=woven[:].rearrange("p c f k -> p c (f k)"),
+                )

@@ -32,19 +32,44 @@ def tile_ginconvfft_pa_s_kernel(tc, x, support, eps, out):
         psum = ctx.enter_context(tc.psum_pool(name="psum", bufs=1))
 
         a_rows = {}
+        x_rows = keep.tile([P, BATCH, PACK, FEAT], BF16)
         for i in range(SUPPORTS):
             by_class = support[i].rearrange("(p c) m -> p c m", c=PACK)
             for half in range(2):
                 classes = slice(half * HALF, (half + 1) * HALF)
                 a_rows[i, half] = keep.tile([P, HALF, NODES], BF16, name="a_rows_%d_%d" % (i, half))
                 nc.sync.dma_start(out=a_rows[i, half][:], in_=by_class[:, classes, :])
-        x_rows = keep.tile([P, BATCH, PACK, FEAT], BF16)
-        nc.scalar.dma_start(out=x_rows[:], in_=x.rearrange("b (p c) l h -> p b c (l h)", c=PACK))
+            if i == 0:
+                nc.sync.dma_start(out=x_rows[:], in_=x.rearrange("b (p c) l h -> p b c (l h)", c=PACK))
         eps_col = keep.tile([P, 1], BF16)
         nc.scalar.dma_start(out=eps_col[:], in_=eps.partition_broadcast(P))
 
         identity = keep.tile([P, P], F32)
         make_identity(nc, identity[:])
+
+        a_codes = {}
+        a_scales = {}
+
+        def quantise_support_half(i, half):
+            words = a_rows[i, half][:].bitcast(F32).rearrange("p c (q u) -> p c q u", u=2)
+            turned = psum.tile([P, HALF, 2, P], F32, name="turned_%d_%d" % (i, half))
+            for c in range(HALF):
+                for u in range(2):
+                    nc.tensor.transpose(turned[:, c, u, :], words[:, c, :, u], identity[:])
+            a_grouped = keep.tile([P, HALF * P, PACK], BF16, align_bytes=64, name="a_grouped_%d_%d" % (i, half))
+            nc.scalar.copy(
+                out=a_grouped[:].bitcast(F32).rearrange("q (c r) u -> q c r u", c=HALF),
+                in_=turned[:].rearrange("q c u r -> q c r u"),
+            )
+            a_codes[i, half] = keep.tile([P, HALF * P], U32, align_bytes=64, name="a_codes_%d_%d" % (i, half))
+            a_scales[i, half] = keep.tile([P, HALF * P], U8, align_bytes=64, name="a_scales_%d_%d" % (i, half))
+            nc.vector.quantize_mx(
+                out=a_codes[i, half][:].bitcast(FP8X4),
+                scales=a_scales[i, half][:],
+                in_=a_grouped[:].rearrange("q w t -> q (w t)"),
+            )
+
+        quantise_support_half(0, 0)
 
         x_grouped = keep.tile([P, COLS, PACK], BF16, align_bytes=64)
         nc.vector.tensor_copy(
@@ -61,27 +86,9 @@ def tile_ginconvfft_pa_s_kernel(tc, x, support, eps, out):
         gain = keep.tile([P, 1], F32)
         nc.vector.tensor_scalar_add(out=gain[:], in0=eps_col[:], scalar1=1.0)
 
-        a_codes = {}
-        a_scales = {}
-        for i in range(SUPPORTS):
-            for half in range(2):
-                words = a_rows[i, half][:].bitcast(F32).rearrange("p c (q u) -> p c q u", u=2)
-                turned = psum.tile([P, HALF, 2, P], F32, name="turned_%d_%d" % (i, half))
-                for c in range(HALF):
-                    for u in range(2):
-                        nc.tensor.transpose(turned[:, c, u, :], words[:, c, :, u], identity[:])
-                a_grouped = keep.tile([P, HALF * P, PACK], BF16, align_bytes=64, name="a_grouped_%d_%d" % (i, half))
-                nc.scalar.copy(
-                    out=a_grouped[:].bitcast(F32).rearrange("q (c r) u -> q c r u", c=HALF),
-                    in_=turned[:].rearrange("q c u r -> q c r u"),
-                )
-                a_codes[i, half] = keep.tile([P, HALF * P], U32, align_bytes=64, name="a_codes_%d_%d" % (i, half))
-                a_scales[i, half] = keep.tile([P, HALF * P], U8, align_bytes=64, name="a_scales_%d_%d" % (i, half))
-                nc.vector.quantize_mx(
-                    out=a_codes[i, half][:].bitcast(FP8X4),
-                    scales=a_scales[i, half][:],
-                    in_=a_grouped[:].rearrange("q w t -> q (w t)"),
-                )
+        quantise_support_half(0, 1)
+        quantise_support_half(1, 0)
+        quantise_support_half(1, 1)
 
         def hop(i, sums, v_codes, v_scales):
             for c in range(PACK):
@@ -130,21 +137,23 @@ def tile_ginconvfft_pa_s_kernel(tc, x, support, eps, out):
                 op1=ADD,
             )
 
+        sums2 = {}
         for i in range(SUPPORTS):
-            sums2 = psum.tile([P, PACK, COLS], F32, name="sums2_%d" % i)
-            hop(i, sums2, h1_codes[i], h1_scales[i])
-            nc.vector.scalar_tensor_tensor(
-                out=results[:, HOPS * i + 1, :, :],
-                in0=results[:, HOPS * i, :, :],
-                scalar=gain[:],
-                in1=sums2[:],
-                op0=MULT,
-                op1=ADD,
-            )
+            sums2[i] = psum.tile([P, PACK, COLS], F32, name="sums2_%d" % i)
+            hop(i, sums2[i], h1_codes[i], h1_scales[i])
 
         out_by_class = out.rearrange("b (p c) l g -> p b c (l g)", c=PACK)
         for half in range(2):
             classes = slice(half * HALF, (half + 1) * HALF)
+            for i in range(SUPPORTS):
+                nc.vector.scalar_tensor_tensor(
+                    out=results[:, HOPS * i + 1, classes, :],
+                    in0=results[:, HOPS * i, classes, :],
+                    scalar=gain[:],
+                    in1=sums2[i][:, classes, :],
+                    op0=MULT,
+                    op1=ADD,
+                )
             for b in range(BATCH):
                 woven = keep.tile([P, HALF, FEAT, RESULTS], F32, name="woven_%d_%d" % (b, half))
                 source = results[:, :, classes, b * FEAT : (b + 1) * FEAT].rearrange("p k c f -> p c f k")

@@ -30,138 +30,143 @@ def tile_ginconvfft_pa_s_kernel(tc, x, support, eps, out):
     with ExitStack() as ctx:
         keep = ctx.enter_context(tc.tile_pool(name="keep", bufs=1))
         psum = ctx.enter_context(tc.psum_pool(name="psum", bufs=1))
+        ctx.enter_context(tc.manual_schedule())
 
         a_rows = {}
         x_rows = keep.tile([P, BATCH, PACK, FEAT], BF16)
-        for i in range(SUPPORTS):
-            by_class = support[i].rearrange("(p c) m -> p c m", c=PACK)
-            for half in range(2):
-                classes = slice(half * HALF, (half + 1) * HALF)
-                a_rows[i, half] = keep.tile([P, HALF, NODES], BF16, name="a_rows_%d_%d" % (i, half))
-                nc.sync.dma_start(out=a_rows[i, half][:], in_=by_class[:, classes, :])
-            if i == 0:
-                nc.sync.dma_start(out=x_rows[:], in_=x.rearrange("b (p c) l h -> p b c (l h)", c=PACK))
+
+        def load_support_half(i, half):
+            classes = slice(half * HALF, (half + 1) * HALF)
+            a_rows[i, half] = keep.tile([P, HALF, NODES], BF16, name="a_rows_%d_%d" % (i, half))
+            nc.sync.dma_start(
+                out=a_rows[i, half][:],
+                in_=support[i].rearrange("(p c) m -> p c m", c=PACK)[:, classes, :],
+            )
+
+        load_support_half(0, 0)
+        nc.sync.dma_start(out=x_rows[:], in_=x.rearrange("b (p c) l h -> p b c (l h)", c=PACK))
+        load_support_half(0, 1)
+        load_support_half(1, 0)
+        load_support_half(1, 1)
         eps_col = keep.tile([P, 1], BF16)
         nc.scalar.dma_start(out=eps_col[:], in_=eps.partition_broadcast(P))
 
         identity = keep.tile([P, P], F32)
         make_identity(nc, identity[:])
 
+        turned = {}
+        a_grouped = {}
         a_codes = {}
         a_scales = {}
 
-        def quantise_support_half(i, half):
-            words = a_rows[i, half][:].bitcast(F32).rearrange("p c (q u) -> p c q u", u=2)
-            turned = psum.tile([P, HALF, 2, P], F32, name="turned_%d_%d" % (i, half))
-            for c in range(HALF):
-                for u in range(2):
-                    nc.tensor.transpose(turned[:, c, u, :], words[:, c, :, u], identity[:])
-            a_grouped = keep.tile([P, HALF * P, PACK], BF16, align_bytes=64, name="a_grouped_%d_%d" % (i, half))
-            nc.scalar.copy(
-                out=a_grouped[:].bitcast(F32).rearrange("q (c r) u -> q c r u", c=HALF),
-                in_=turned[:].rearrange("q c u r -> q c r u"),
-            )
-            a_codes[i, half] = keep.tile([P, HALF * P], U32, align_bytes=64, name="a_codes_%d_%d" % (i, half))
-            a_scales[i, half] = keep.tile([P, HALF * P], U8, align_bytes=64, name="a_scales_%d_%d" % (i, half))
-            nc.vector.quantize_mx(
-                out=a_codes[i, half][:].bitcast(FP8X4),
-                scales=a_scales[i, half][:],
-                in_=a_grouped[:].rearrange("q w t -> q (w t)"),
+        def turn(i, c):
+            words = a_rows[i, c // HALF][:, c % HALF, :].bitcast(F32).rearrange("p (q u) -> p q u", u=2)
+            turned[i, c] = psum.tile([P, 2, P], F32, tag="bank", bufs=6, name="turned_%d_%d" % (i, c))
+            for u in range(2):
+                nc.tensor.transpose(turned[i, c][:, u, :], words[:, :, u], identity[:])
+
+        def group(i, c, copy=nc.scalar.copy):
+            a_grouped[i, c] = keep.tile([P, P, PACK], BF16, align_bytes=64, name="a_grouped_%d_%d" % (i, c))
+            copy(
+                out=a_grouped[i, c][:].bitcast(F32),
+                in_=turned[i, c][:].rearrange("q u r -> q r u"),
             )
 
-        quantise_support_half(0, 0)
+        def quantise(in_, codes, scales):
+            nc.vector.quantize_mx(
+                out=codes[:].bitcast(FP8X4), scales=scales[:], in_=in_[:].rearrange("p w t -> p (w t)")
+            )
+
+        def quantise_support(i, c):
+            a_codes[i, c] = keep.tile([P, P], U32, align_bytes=64, name="a_codes_%d_%d" % (i, c))
+            a_scales[i, c] = keep.tile([P, P], U8, align_bytes=64, name="a_scales_%d_%d" % (i, c))
+            quantise(a_grouped[i, c], a_codes[i, c], a_scales[i, c])
+
+        def multiply(sums, i, c, v):
+            nc.tensor.matmul_mx(
+                out=sums,
+                lhsT=a_codes[i, c][:].bitcast(FP8X4),
+                lhsT_scale=a_scales[i, c][:],
+                rhs=v[0][:].bitcast(FP8X4),
+                rhs_scale=v[1][:],
+                start=True,
+                stop=True,
+            )
+
+        def self_plus(out_, in0, in1):
+            nc.vector.scalar_tensor_tensor(out=out_, in0=in0, scalar=gain[:], in1=in1, op0=MULT, op1=ADD)
 
         x_grouped = keep.tile([P, COLS, PACK], BF16, align_bytes=64)
+        x_codes = keep.tile([P, COLS], U32, align_bytes=64)
+        x_scales = keep.tile([P, COLS], U8, align_bytes=64)
+        gain = keep.tile([P, 1], F32)
+        base = keep.tile([P, RESULTS, PACK, COLS], F32)
+        h1_grouped = {}
+        h1_codes = {}
+        h1_scales = {}
+        sums1 = {}
+        for i in range(SUPPORTS):
+            h1_grouped[i] = keep.tile([P, COLS, PACK], BF16, align_bytes=64, name="h1_grouped_%d" % i)
+            h1_codes[i] = keep.tile([P, COLS], U32, align_bytes=64, name="h1_codes_%d" % i)
+            h1_scales[i] = keep.tile([P, COLS], U8, align_bytes=64, name="h1_scales_%d" % i)
+            sums1[i] = psum.tile([P, PACK, COLS], F32, name="sums1_%d" % i)
+        xv = (x_codes, x_scales)
+
+        for c in range(PACK):
+            turn(0, c)
+        group(0, 0)
         nc.vector.tensor_copy(
             out=x_grouped[:].rearrange("p (b f) c -> p b f c", b=BATCH),
             in_=x_rows[:].rearrange("p b c f -> p b f c"),
         )
-        x_codes = keep.tile([P, COLS], U32, align_bytes=64)
-        x_scales = keep.tile([P, COLS], U8, align_bytes=64)
-        nc.vector.quantize_mx(
-            out=x_codes[:].bitcast(FP8X4),
-            scales=x_scales[:],
-            in_=x_grouped[:].rearrange("p w c -> p (w c)"),
-        )
-        gain = keep.tile([P, 1], F32)
         nc.vector.tensor_scalar_add(out=gain[:], in0=eps_col[:], scalar1=1.0)
+        group(0, 1, nc.vector.tensor_copy)
+        quantise(x_grouped, x_codes, x_scales)
+        group(0, 2)
+        group(0, 3)
+        for c in range(PACK):
+            quantise_support(0, c)
+        for c in range(3):
+            turn(1, c)
+            group(1, c)
+        for c in range(PACK):
+            multiply(sums1[0][:, c, :], 0, c, xv)
+        turn(1, 3)
+        group(1, 3)
+        quantise_support(1, 0)
+        quantise_support(1, 1)
+        self_plus(base[:, 1, :, :], x_grouped[:].rearrange("p w c -> p c w"), sums1[0][:])
+        quantise_support(1, 2)
+        quantise_support(1, 3)
+        nc.scalar.copy(out=h1_grouped[0][:], in_=base[:, 1, :, :].rearrange("p c w -> p w c"))
+        sums = {}
+        for c in range(PACK):
+            sums[c] = psum.tile([P, RESULTS, COLS], F32, tag="bank", bufs=6, name="sums_%d" % c)
+            multiply(sums[c][:, 0, :], 0, c, xv)
+        for c in range(PACK):
+            multiply(sums1[1][:, c, :], 1, c, xv)
+        self_plus(h1_grouped[1][:], x_grouped[:], sums1[1][:].rearrange("p c w -> p w c"))
+        for c in range(PACK):
+            multiply(sums[c][:, 2, :], 1, c, xv)
+        quantise(h1_grouped[0], h1_codes[0], h1_scales[0])
+        quantise(h1_grouped[1], h1_codes[1], h1_scales[1])
+        self_plus(base[:, 3, :, :], x_grouped[:].rearrange("p w c -> p c w"), sums1[1][:])
+        for k in (0, 2):
+            nc.scalar.copy(out=base[:, k, :, :], in_=x_grouped[:].rearrange("p w c -> p c w"))
 
-        quantise_support_half(0, 1)
-        quantise_support_half(1, 0)
-        quantise_support_half(1, 1)
-
-        def hop(i, sums, v_codes, v_scales):
+        for i in range(SUPPORTS):
             for c in range(PACK):
-                half = c // HALF
-                rows = slice((c % HALF) * P, (c % HALF + 1) * P)
-                nc.tensor.matmul_mx(
-                    out=sums[:, c, :],
-                    lhsT=a_codes[i, half][:, rows].bitcast(FP8X4),
-                    lhsT_scale=a_scales[i, half][:, rows],
-                    rhs=v_codes[:].bitcast(FP8X4),
-                    rhs_scale=v_scales[:],
-                    start=True,
-                    stop=True,
-                )
+                multiply(sums[c][:, HOPS * i + 1, :], i, c, (h1_codes[i], h1_scales[i]))
 
-        results = keep.tile([P, RESULTS, PACK, COLS], F32)
-
-        sums1 = {}
-        h1_codes = {}
-        h1_scales = {}
-        for i in range(SUPPORTS):
-            sums1[i] = psum.tile([P, PACK, COLS], F32, name="sums1_%d" % i)
-            hop(i, sums1[i], x_codes, x_scales)
-            h1_grouped = keep.tile([P, COLS, PACK], BF16, align_bytes=64, name="h1_grouped_%d" % i)
-            nc.vector.scalar_tensor_tensor(
-                out=h1_grouped[:],
-                in0=x_grouped[:],
-                scalar=gain[:],
-                in1=sums1[i][:].rearrange("p c w -> p w c"),
-                op0=MULT,
-                op1=ADD,
+        out_by_class = out.rearrange("b (p c) l g -> p c b (l g)", c=PACK)
+        for c in range(PACK):
+            woven = keep.tile([P, COLS, RESULTS], F32, name="woven_%d" % c)
+            self_plus(
+                woven[:],
+                base[:, :, c, :].rearrange("p k w -> p w k"),
+                sums[c][:].rearrange("p k w -> p w k"),
             )
-            h1_codes[i] = keep.tile([P, COLS], U32, align_bytes=64, name="h1_codes_%d" % i)
-            h1_scales[i] = keep.tile([P, COLS], U8, align_bytes=64, name="h1_scales_%d" % i)
-            nc.vector.quantize_mx(
-                out=h1_codes[i][:].bitcast(FP8X4),
-                scales=h1_scales[i][:],
-                in_=h1_grouped[:].rearrange("p w c -> p (w c)"),
+            nc.sync.dma_start(
+                out=out_by_class[:, c, :, :],
+                in_=woven[:].rearrange("p (b f) k -> p b (f k)", b=BATCH),
             )
-            nc.vector.scalar_tensor_tensor(
-                out=results[:, HOPS * i, :, :],
-                in0=x_grouped[:].rearrange("p w c -> p c w"),
-                scalar=gain[:],
-                in1=sums1[i][:],
-                op0=MULT,
-                op1=ADD,
-            )
-
-        sums2 = {}
-        for i in range(SUPPORTS):
-            sums2[i] = psum.tile([P, PACK, COLS], F32, name="sums2_%d" % i)
-            hop(i, sums2[i], h1_codes[i], h1_scales[i])
-
-        out_by_class = out.rearrange("b (p c) l g -> p b c (l g)", c=PACK)
-        for half in range(2):
-            classes = slice(half * HALF, (half + 1) * HALF)
-            for i in range(SUPPORTS):
-                nc.vector.scalar_tensor_tensor(
-                    out=results[:, HOPS * i + 1, classes, :],
-                    in0=results[:, HOPS * i, classes, :],
-                    scalar=gain[:],
-                    in1=sums2[i][:, classes, :],
-                    op0=MULT,
-                    op1=ADD,
-                )
-            for b in range(BATCH):
-                woven = keep.tile([P, HALF, FEAT, RESULTS], F32, name="woven_%d_%d" % (b, half))
-                source = results[:, :, classes, b * FEAT : (b + 1) * FEAT].rearrange("p k c f -> p c f k")
-                if b == 0:
-                    nc.vector.tensor_copy(out=woven[:], in_=source)
-                else:
-                    nc.scalar.copy(out=woven[:], in_=source)
-                nc.sync.dma_start(
-                    out=out_by_class[:, b, classes, :],
-                    in_=woven[:].rearrange("p c f k -> p c (f k)"),
-                )

@@ -54,6 +54,12 @@ def tile_ginconvfft_pa_s_kernel(tc, x, support, eps, out):
         identity = keep.tile([P, P], F32)
         make_identity(nc, identity[:])
 
+        zeros = keep.tile([P, 2 * P], F32)
+        nc.vector.memset(zeros[:], 0.0)
+        warm = psum.tile([P, 2 * P], F32)
+        for n in range(2):
+            nc.tensor.matmul(warm[:], lhsT=zeros[:, :P], rhs=zeros[:], start=True, stop=True)
+
         turned = {}
         a_grouped = {}
         a_codes = {}
@@ -61,7 +67,7 @@ def tile_ginconvfft_pa_s_kernel(tc, x, support, eps, out):
 
         def turn(i, c):
             words = a_rows[i, c // HALF][:, c % HALF, :].bitcast(F32).rearrange("p (q u) -> p q u", u=2)
-            turned[i, c] = psum.tile([P, 2, P], F32, tag="bank", bufs=6, name="turned_%d_%d" % (i, c))
+            turned[i, c] = psum.tile([P, 2, P], F32, tag="bank", bufs=5, name="turned_%d_%d" % (i, c))
             for u in range(2):
                 nc.tensor.transpose(turned[i, c][:, u, :], words[:, :, u], identity[:])
 
@@ -141,7 +147,7 @@ def tile_ginconvfft_pa_s_kernel(tc, x, support, eps, out):
         nc.scalar.copy(out=h1_grouped[0][:], in_=base[:, 1, :, :].rearrange("p c w -> p w c"))
         sums = {}
         for c in range(PACK):
-            sums[c] = psum.tile([P, RESULTS, COLS], F32, tag="bank", bufs=6, name="sums_%d" % c)
+            sums[c] = psum.tile([P, RESULTS, COLS], F32, tag="bank", bufs=5, name="sums_%d" % c)
             multiply(sums[c][:, 0, :], 0, c, xv)
         for c in range(PACK):
             multiply(sums1[1][:, c, :], 1, c, xv)

@@ -48,17 +48,21 @@ def tile_ginconvfft_pa_s_kernel(tc, x, support, eps, out):
         load_support_half(0, 1)
         load_support_half(1, 0)
         load_support_half(1, 1)
-        eps_col = keep.tile([P, 1], BF16)
-        nc.scalar.dma_start(out=eps_col[:], in_=eps.partition_broadcast(P))
 
         identity = keep.tile([P, P], F32)
         make_identity(nc, identity[:])
 
         zeros = keep.tile([P, 2 * P], F32)
         nc.vector.memset(zeros[:], 0.0)
-        warm = psum.tile([P, 2 * P], F32)
+        eps_col = keep.tile([P, 2], BF16)
+        nc.vector.memset(eps_col[:], 0.0)
+        nc.scalar.dma_start(out=eps_col[0:1, 0:1], in_=eps.unsqueeze(0))
+        ones = keep.tile([P, P], BF16)
+        nc.vector.memset(ones[:], 1.0)
+        warm = psum.tile([P, 2 * P], F32, tag="spare")
         for n in range(2):
             nc.tensor.matmul(warm[:], lhsT=zeros[:, :P], rhs=zeros[:], start=True, stop=True)
+        eps_all = psum.tile([P, 2], F32, tag="spare")
 
         turned = {}
         a_grouped = {}
@@ -120,18 +124,19 @@ def tile_ginconvfft_pa_s_kernel(tc, x, support, eps, out):
 
         for c in range(PACK):
             turn(0, c)
+        nc.tensor.matmul(eps_all[:], lhsT=ones[:], rhs=eps_col[:], start=True, stop=True)
         group(0, 0)
         nc.vector.tensor_copy(
             out=x_grouped[:].rearrange("p (b f) c -> p b f c", b=BATCH),
             in_=x_rows[:].rearrange("p b c f -> p b f c"),
         )
-        nc.vector.tensor_scalar_add(out=gain[:], in0=eps_col[:], scalar1=1.0)
         group(0, 1, nc.vector.tensor_copy)
         quantise(x_grouped, x_codes, x_scales)
         group(0, 2)
         group(0, 3)
         for c in range(PACK):
             quantise_support(0, c)
+        nc.vector.tensor_scalar_add(out=gain[:], in0=eps_all[:, 0:1], scalar1=1.0)
         for c in range(3):
             turn(1, c)
             group(1, c)

@@ -52,10 +52,10 @@ def tile_ginconvfft_pa_s_kernel(tc, x, support, eps, out):
         identity = keep.tile([P, P], F32)
         make_identity(nc, identity[:])
 
-        zeros = keep.tile([P, 2 * P], F32)
-        nc.vector.memset(zeros[:], 0.0)
         eps_col = keep.tile([P, 2], BF16)
         nc.vector.memset(eps_col[:], 0.0)
+        zeros = keep.tile([P, 2 * P], F32)
+        nc.vector.memset(zeros[:], 0.0)
         nc.scalar.dma_start(out=eps_col[0:1, 0:1], in_=eps.unsqueeze(0))
         ones = keep.tile([P, P], BF16)
         nc.vector.memset(ones[:], 1.0)
@@ -124,7 +124,6 @@ def tile_ginconvfft_pa_s_kernel(tc, x, support, eps, out):
 
         for c in range(PACK):
             turn(0, c)
-        nc.tensor.matmul(eps_all[:], lhsT=ones[:], rhs=eps_col[:], start=True, stop=True)
         group(0, 0)
         nc.vector.tensor_copy(
             out=x_grouped[:].rearrange("p (b f) c -> p b f c", b=BATCH),
@@ -136,15 +135,16 @@ def tile_ginconvfft_pa_s_kernel(tc, x, support, eps, out):
         group(0, 3)
         for c in range(PACK):
             quantise_support(0, c)
-        nc.vector.tensor_scalar_add(out=gain[:], in0=eps_all[:, 0:1], scalar1=1.0)
         for c in range(3):
             turn(1, c)
             group(1, c)
+        nc.tensor.matmul(eps_all[:], lhsT=ones[:], rhs=eps_col[:], start=True, stop=True)
         for c in range(PACK):
             multiply(sums1[0][:, c, :], 0, c, xv)
         turn(1, 3)
         group(1, 3)
         quantise_support(1, 0)
+        nc.vector.tensor_scalar_add(out=gain[:], in0=eps_all[:, 0:1], scalar1=1.0)
         quantise_support(1, 1)
         self_plus(base[:, 1, :, :], x_grouped[:].rearrange("p w c -> p c w"), sums1[0][:])
         quantise_support(1, 2)
@@ -165,8 +165,8 @@ def tile_ginconvfft_pa_s_kernel(tc, x, support, eps, out):
         for k in (0, 2):
             nc.scalar.copy(out=base[:, k, :, :], in_=x_grouped[:].rearrange("p w c -> p c w"))
 
-        for i in range(SUPPORTS):
-            for c in range(PACK):
+        for c in range(PACK):
+            for i in range(SUPPORTS):
                 multiply(sums[c][:, HOPS * i + 1, :], i, c, (h1_codes[i], h1_scales[i]))
 
         out_by_class = out.rearrange("b (p c) l g -> p c b (l g)", c=PACK)

@@ -36,15 +36,18 @@ def tile_ginconvfft_pa_s_kernel(tc, x, support, eps, out):
         x_rows = keep.tile([P, BATCH, PACK, FEAT], BF16)
 
         def load_support_half(i, half):
-            classes = slice(half * HALF, (half + 1) * HALF)
             a_rows[i, half] = keep.tile([P, HALF, NODES], BF16, name="a_rows_%d_%d" % (i, half))
             nc.sync.dma_start(
                 out=a_rows[i, half][:],
-                in_=support[i].rearrange("(p c) m -> p c m", c=PACK)[:, classes, :],
+                in_=support[i].rearrange("(u p e) m -> u p e m", u=2, e=HALF)[half],
             )
 
         load_support_half(0, 0)
-        nc.sync.dma_start(out=x_rows[:], in_=x.rearrange("b (p c) l h -> p b c (l h)", c=PACK))
+        for u in range(2):
+            nc.sync.dma_start(
+                out=x_rows[:, :, u * HALF : (u + 1) * HALF, :].rearrange("p b e f -> p b (e f)"),
+                in_=x.rearrange("b (u p e) l h -> u p b (e l h)", u=2, e=HALF)[u],
+            )
         load_support_half(0, 1)
         load_support_half(1, 0)
         load_support_half(1, 1)
@@ -70,10 +73,10 @@ def tile_ginconvfft_pa_s_kernel(tc, x, support, eps, out):
         a_scales = {}
 
         def turn(i, c):
-            words = a_rows[i, c // HALF][:, c % HALF, :].bitcast(F32).rearrange("p (q u) -> p q u", u=2)
+            words = a_rows[i, c // HALF][:, c % HALF, :].bitcast(F32)
             turned[i, c] = psum.tile([P, 2, P], F32, tag="bank", bufs=5, name="turned_%d_%d" % (i, c))
             for u in range(2):
-                nc.tensor.transpose(turned[i, c][:, u, :], words[:, :, u], identity[:])
+                nc.tensor.transpose(turned[i, c][:, u, :], words[:, u * P : (u + 1) * P], identity[:])
 
         def group(i, c, copy=nc.scalar.copy):
             a_grouped[i, c] = keep.tile([P, P, PACK], BF16, align_bytes=64, name="a_grouped_%d_%d" % (i, c))
@@ -169,7 +172,7 @@ def tile_ginconvfft_pa_s_kernel(tc, x, support, eps, out):
             for i in range(SUPPORTS):
                 multiply(sums[c][:, HOPS * i + 1, :], i, c, (h1_codes[i], h1_scales[i]))
 
-        out_by_class = out.rearrange("b (p c) l g -> p c b (l g)", c=PACK)
+        out_by_class = out.rearrange("b (u p e) l g -> u e p b (l g)", u=2, e=HALF)
         for c in range(PACK):
             woven = keep.tile([P, COLS, RESULTS], F32, name="woven_%d" % c)
             self_plus(
@@ -178,6 +181,6 @@ def tile_ginconvfft_pa_s_kernel(tc, x, support, eps, out):
                 sums[c][:].rearrange("p k w -> p w k"),
             )
             nc.sync.dma_start(
-                out=out_by_class[:, c, :, :],
+                out=out_by_class[c // HALF, c % HALF],
                 in_=woven[:].rearrange("p (b f) k -> p b (f k)", b=BATCH),
             )

@@ -55,16 +55,17 @@ def tile_ginconvfft_pa_s_kernel(tc, x, support, eps, out):
         identity = keep.tile([P, P], F32)
         make_identity(nc, identity[:])
 
+        zero = keep.tile([P, 1], F32)
+        nc.vector.memset(zero[:], 0.0)
+        warm = psum.tile([P, NODES], F32, tag="spare")
+        nc.tensor.matmul(
+            warm[:], lhsT=zero[:].to_broadcast([P, P]), rhs=zero[:].to_broadcast([P, NODES]), start=True, stop=True
+        )
         eps_col = keep.tile([P, 2], BF16)
         nc.vector.memset(eps_col[:], 0.0)
-        zeros = keep.tile([P, 2 * P], F32)
-        nc.vector.memset(zeros[:], 0.0)
         nc.scalar.dma_start(out=eps_col[0:1, 0:1], in_=eps.unsqueeze(0))
         ones = keep.tile([P, P], BF16)
         nc.vector.memset(ones[:], 1.0)
-        warm = psum.tile([P, 2 * P], F32, tag="spare")
-        for n in range(2):
-            nc.tensor.matmul(warm[:], lhsT=zeros[:, :P], rhs=zeros[:], start=True, stop=True)
         eps_all = psum.tile([P, 2], F32, tag="spare")
 
         turned = {}
@@ -164,7 +165,6 @@ def tile_ginconvfft_pa_s_kernel(tc, x, support, eps, out):
             multiply(sums[c][:, 2, :], 1, c, xv)
         quantise(h1_grouped[0], h1_codes[0], h1_scales[0])
         quantise(h1_grouped[1], h1_codes[1], h1_scales[1])
-        self_plus(base[:, 3, :, :], x_grouped[:].rearrange("p w c -> p c w"), sums1[1][:])
         for k in (0, 2):
             nc.scalar.copy(out=base[:, k, :, :], in_=x_grouped[:].rearrange("p w c -> p c w"))
 
@@ -173,7 +173,14 @@ def tile_ginconvfft_pa_s_kernel(tc, x, support, eps, out):
                 multiply(sums[c][:, HOPS * i + 1, :], i, c, (h1_codes[i], h1_scales[i]))
 
         out_by_class = out.rearrange("b (u p e) l g -> u e p b (l g)", u=2, e=HALF)
+
+        def keep_h1(c):
+            self_plus(base[:, 3, c, :], x_grouped[:, :, c], sums1[1][:, c, :])
+
+        keep_h1(0)
         for c in range(PACK):
+            if c + 1 < PACK:
+                keep_h1(c + 1)
             woven = keep.tile([P, COLS, RESULTS], F32, name="woven_%d" % c)
             self_plus(
                 woven[:],

@@ -58,15 +58,23 @@ def tile_ginconvfft_pa_s_kernel(tc, x, support, eps, out):
         zero = keep.tile([P, 1], F32)
         nc.vector.memset(zero[:], 0.0)
         warm = psum.tile([P, NODES], F32, tag="spare")
-        nc.tensor.matmul(
-            warm[:], lhsT=zero[:].to_broadcast([P, P]), rhs=zero[:].to_broadcast([P, NODES]), start=True, stop=True
-        )
+
+        def load_tensor(n):
+            nc.tensor.matmul(
+                warm[:, :n],
+                lhsT=zero[:].to_broadcast([P, P]),
+                rhs=zero[:].to_broadcast([P, n]),
+                start=True,
+                stop=True,
+            )
+
+        load_tensor(NODES)
         eps_col = keep.tile([P, 2], BF16)
         nc.vector.memset(eps_col[:], 0.0)
         nc.scalar.dma_start(out=eps_col[0:1, 0:1], in_=eps.unsqueeze(0))
         ones = keep.tile([P, P], BF16)
         nc.vector.memset(ones[:], 1.0)
-        eps_all = psum.tile([P, 2], F32, tag="spare")
+        eps_all = warm[:, :2]
 
         turned = {}
         a_grouped = {}
@@ -128,6 +136,8 @@ def tile_ginconvfft_pa_s_kernel(tc, x, support, eps, out):
 
         for c in range(PACK):
             turn(0, c)
+            if c % HALF == 1:
+                load_tensor(P)
         group(0, 0)
         nc.vector.tensor_copy(
             out=x_grouped[:].rearrange("p (b f) c -> p b f c", b=BATCH),
@@ -142,7 +152,7 @@ def tile_ginconvfft_pa_s_kernel(tc, x, support, eps, out):
         for c in range(3):
             turn(1, c)
             group(1, c)
-        nc.tensor.matmul(eps_all[:], lhsT=ones[:], rhs=eps_col[:], start=True, stop=True)
+        nc.tensor.matmul(eps_all, lhsT=ones[:], rhs=eps_col[:], start=True, stop=True)
         for c in range(PACK):
             multiply(sums1[0][:, c, :], 0, c, xv)
         turn(1, 3)

@@ -134,6 +134,13 @@ def tile_ginconvfft_pa_s_kernel(tc, x, support, eps, out):
             sums1[i] = psum.tile([P, PACK, COLS], F32, name="sums1_%d" % i)
         xv = (x_codes, x_scales)
 
+        def keep_h1(i, classes, cols=slice(0, COLS)):
+            self_plus(
+                base[:, HOPS * i + 1, classes, cols],
+                x_grouped[:, cols, classes].rearrange("p w c -> p c w"),
+                sums1[i][:, classes, cols],
+            )
+
         for c in range(PACK):
             turn(0, c)
             if c % HALF == 1:
@@ -149,21 +156,24 @@ def tile_ginconvfft_pa_s_kernel(tc, x, support, eps, out):
         group(0, 3)
         for c in range(PACK):
             quantise_support(0, c)
-        for c in range(3):
+        for c in range(PACK):
             turn(1, c)
             group(1, c)
         nc.tensor.matmul(eps_all, lhsT=ones[:], rhs=eps_col[:], start=True, stop=True)
         for c in range(PACK):
             multiply(sums1[0][:, c, :], 0, c, xv)
-        turn(1, 3)
-        group(1, 3)
         quantise_support(1, 0)
         nc.vector.tensor_scalar_add(out=gain[:], in0=eps_all[:, 0:1], scalar1=1.0)
         quantise_support(1, 1)
-        self_plus(base[:, 1, :, :], x_grouped[:].rearrange("p w c -> p c w"), sums1[0][:])
         quantise_support(1, 2)
-        quantise_support(1, 3)
-        nc.scalar.copy(out=h1_grouped[0][:], in_=base[:, 1, :, :].rearrange("p c w -> p w c"))
+        nc.scalar.copy(out=base[:, 0, :, :], in_=x_grouped[:].rearrange("p w c -> p c w"))
+        for b in range(BATCH):
+            cols = slice(b * FEAT, (b + 1) * FEAT)
+            keep_h1(0, slice(0, PACK), cols)
+            if b == 0:
+                quantise_support(1, 3)
+            nc.scalar.copy(out=h1_grouped[0][:, cols, :], in_=base[:, 1, :, cols].rearrange("p c w -> p w c"))
+        nc.scalar.copy(out=base[:, 2, :, :], in_=x_grouped[:].rearrange("p w c -> p c w"))
         sums = {}
         for c in range(PACK):
             sums[c] = psum.tile([P, RESULTS, COLS], F32, tag="bank", bufs=5, name="sums_%d" % c)
@@ -173,24 +183,17 @@ def tile_ginconvfft_pa_s_kernel(tc, x, support, eps, out):
         self_plus(h1_grouped[1][:], x_grouped[:], sums1[1][:].rearrange("p c w -> p w c"))
         for c in range(PACK):
             multiply(sums[c][:, 2, :], 1, c, xv)
-        quantise(h1_grouped[0], h1_codes[0], h1_scales[0])
-        quantise(h1_grouped[1], h1_codes[1], h1_scales[1])
-        for k in (0, 2):
-            nc.scalar.copy(out=base[:, k, :, :], in_=x_grouped[:].rearrange("p w c -> p c w"))
-
+        keep_h1(1, slice(0, 1))
+        for i in (1, 0):
+            quantise(h1_grouped[i], h1_codes[i], h1_scales[i])
+        keep_h1(1, slice(1, PACK))
         for c in range(PACK):
-            for i in range(SUPPORTS):
+            for i in (1, 0):
                 multiply(sums[c][:, HOPS * i + 1, :], i, c, (h1_codes[i], h1_scales[i]))
 
         out_by_class = out.rearrange("b (u p e) l g -> u e p b (l g)", u=2, e=HALF)
 
-        def keep_h1(c):
-            self_plus(base[:, 3, c, :], x_grouped[:, :, c], sums1[1][:, c, :])
-
-        keep_h1(0)
         for c in range(PACK):
-            if c + 1 < PACK:
-                keep_h1(c + 1)
             woven = keep.tile([P, COLS, RESULTS], F32, name="woven_%d" % c)
             self_plus(
                 woven[:],

@@ -164,14 +164,12 @@ def tile_ginconvfft_pa_s_kernel(tc, x, support, eps, out):
             multiply(sums1[0][:, c, :], 0, c, xv)
         quantise_support(1, 0)
         nc.vector.tensor_scalar_add(out=gain[:], in0=eps_all[:, 0:1], scalar1=1.0)
-        quantise_support(1, 1)
-        quantise_support(1, 2)
+        for c in range(1, PACK):
+            quantise_support(1, c)
         nc.scalar.copy(out=base[:, 0, :, :], in_=x_grouped[:].rearrange("p w c -> p c w"))
         for b in range(BATCH):
             cols = slice(b * FEAT, (b + 1) * FEAT)
             keep_h1(0, slice(0, PACK), cols)
-            if b == 0:
-                quantise_support(1, 3)
             nc.scalar.copy(out=h1_grouped[0][:, cols, :], in_=base[:, 1, :, cols].rearrange("p c w -> p w c"))
         nc.scalar.copy(out=base[:, 2, :, :], in_=x_grouped[:].rearrange("p w c -> p c w"))
         sums = {}

@@ -35,22 +35,23 @@ def tile_ginconvfft_pa_s_kernel(tc, x, support, eps, out):
         a_rows = {}
         x_rows = keep.tile([P, BATCH, PACK, FEAT], BF16)
 
-        def load_support_half(i, half):
-            a_rows[i, half] = keep.tile([P, HALF, NODES], BF16, name="a_rows_%d_%d" % (i, half))
-            nc.sync.dma_start(
-                out=a_rows[i, half][:],
-                in_=support[i].rearrange("(u p e) m -> u p e m", u=2, e=HALF)[half],
-            )
+        def load_support(i, first, end):
+            rows = keep.tile([P, end - first, NODES], BF16, name="a_rows_%d_%d" % (i, first))
+            by_half = support[i].rearrange("(u p e) m -> u p e m", u=2, e=HALF)[first // HALF]
+            nc.sync.dma_start(out=rows[:], in_=by_half[:, first % HALF : first % HALF + end - first, :])
+            for c in range(first, end):
+                a_rows[i, c] = rows[:, c - first, :]
 
-        load_support_half(0, 0)
+        load_support(0, 0, 2)
         for u in range(2):
             nc.sync.dma_start(
                 out=x_rows[:, :, u * HALF : (u + 1) * HALF, :].rearrange("p b e f -> p b (e f)"),
                 in_=x.rearrange("b (u p e) l h -> u p b (e l h)", u=2, e=HALF)[u],
             )
-        load_support_half(0, 1)
-        load_support_half(1, 0)
-        load_support_half(1, 1)
+        load_support(0, 2, 4)
+        load_support(1, 0, 2)
+        load_support(1, 2, 3)
+        load_support(1, 3, 4)
 
         identity = keep.tile([P, P], F32)
         make_identity(nc, identity[:])
@@ -82,7 +83,7 @@ def tile_ginconvfft_pa_s_kernel(tc, x, support, eps, out):
         a_scales = {}
 
         def turn(i, c):
-            words = a_rows[i, c // HALF][:, c % HALF, :].bitcast(F32)
+            words = a_rows[i, c].bitcast(F32)
             turned[i, c] = psum.tile([P, 2, P], F32, tag="bank", bufs=5, name="turned_%d_%d" % (i, c))
             for u in range(2):
                 nc.tensor.transpose(turned[i, c][:, u, :], words[:, u * P : (u + 1) * P], identity[:])

@@ -49,7 +49,8 @@ def tile_ginconvfft_pa_s_kernel(tc, x, support, eps, out):
                 in_=x.rearrange("b (u p e) l h -> u p b (e l h)", u=2, e=HALF)[u],
             )
         load_support(0, 2, 4)
-        load_support(1, 0, 2)
+        load_support(1, 0, 1)
+        load_support(1, 1, 2)
         load_support(1, 2, 3)
         load_support(1, 3, 4)
 
@@ -88,28 +89,32 @@ def tile_ginconvfft_pa_s_kernel(tc, x, support, eps, out):
             for u in range(2):
                 nc.tensor.transpose(turned[i, c][:, u, :], words[:, u * P : (u + 1) * P], identity[:])
 
+        for i in range(SUPPORTS):
+            for half in range(2):
+                a_grouped[i, half] = keep.tile([P, HALF * P, PACK], BF16, align_bytes=64, name="a_grouped_%d_%d" % (i, half))
+                a_codes[i, half] = keep.tile([P, HALF * P], U32, align_bytes=64, name="a_codes_%d_%d" % (i, half))
+                a_scales[i, half] = keep.tile([P, HALF * P], U8, align_bytes=64, name="a_scales_%d_%d" % (i, half))
+
+        def in_half(c):
+            return slice((c % HALF) * P, (c % HALF + 1) * P)
+
         def group(i, c, copy=nc.scalar.copy):
-            a_grouped[i, c] = keep.tile([P, P, PACK], BF16, align_bytes=64, name="a_grouped_%d_%d" % (i, c))
             copy(
-                out=a_grouped[i, c][:].bitcast(F32),
+                out=a_grouped[i, c // HALF][:, in_half(c), :].bitcast(F32),
                 in_=turned[i, c][:].rearrange("q u r -> q r u"),
             )
 
         def quantise(in_, codes, scales):
-            nc.vector.quantize_mx(
-                out=codes[:].bitcast(FP8X4), scales=scales[:], in_=in_[:].rearrange("p w t -> p (w t)")
-            )
+            nc.vector.quantize_mx(out=codes.bitcast(FP8X4), scales=scales, in_=in_.rearrange("p w t -> p (w t)"))
 
-        def quantise_support(i, c):
-            a_codes[i, c] = keep.tile([P, P], U32, align_bytes=64, name="a_codes_%d_%d" % (i, c))
-            a_scales[i, c] = keep.tile([P, P], U8, align_bytes=64, name="a_scales_%d_%d" % (i, c))
-            quantise(a_grouped[i, c], a_codes[i, c], a_scales[i, c])
+        def quantise_support(i, half, rows=slice(0, HALF * P)):
+            quantise(a_grouped[i, half][:, rows, :], a_codes[i, half][:, rows], a_scales[i, half][:, rows])
 
         def multiply(sums, i, c, v):
             nc.tensor.matmul_mx(
                 out=sums,
-                lhsT=a_codes[i, c][:].bitcast(FP8X4),
-                lhsT_scale=a_scales[i, c][:],
+                lhsT=a_codes[i, c // HALF][:, in_half(c)].bitcast(FP8X4),
+                lhsT_scale=a_scales[i, c // HALF][:, in_half(c)],
                 rhs=v[0][:].bitcast(FP8X4),
                 rhs_scale=v[1][:],
                 start=True,
@@ -144,29 +149,31 @@ def tile_ginconvfft_pa_s_kernel(tc, x, support, eps, out):
 
         for c in range(PACK):
             turn(0, c)
-            if c % HALF == 1:
-                load_tensor(P)
+            if c == 1:
+                load_tensor(160)
         group(0, 0)
         nc.vector.tensor_copy(
             out=x_grouped[:].rearrange("p (b f) c -> p b f c", b=BATCH),
             in_=x_rows[:].rearrange("p b c f -> p b f c"),
         )
-        group(0, 1, nc.vector.tensor_copy)
-        quantise(x_grouped, x_codes, x_scales)
+        group(0, 1)
+        quantise(x_grouped[:], x_codes[:], x_scales[:])
         group(0, 2)
-        group(0, 3)
-        for c in range(PACK):
-            quantise_support(0, c)
+        quantise_support(0, 0)
+        group(0, 3, nc.vector.tensor_copy)
+        quantise_support(0, 1)
         for c in range(PACK):
             turn(1, c)
+            if c == 1:
+                load_tensor(P)
             group(1, c)
         nc.tensor.matmul(eps_all, lhsT=ones[:], rhs=eps_col[:], start=True, stop=True)
         for c in range(PACK):
             multiply(sums1[0][:, c, :], 0, c, xv)
         quantise_support(1, 0)
         nc.vector.tensor_scalar_add(out=gain[:], in0=eps_all[:, 0:1], scalar1=1.0)
-        for c in range(1, PACK):
-            quantise_support(1, c)
+        for c in (2, 3):
+            quantise_support(1, 1, in_half(c))
         nc.scalar.copy(out=base[:, 0, :, :], in_=x_grouped[:].rearrange("p w c -> p c w"))
         for b in range(BATCH):
             cols = slice(b * FEAT, (b + 1) * FEAT)
@@ -184,7 +191,7 @@ def tile_ginconvfft_pa_s_kernel(tc, x, support, eps, out):
             multiply(sums[c][:, 2, :], 1, c, xv)
         keep_h1(1, slice(0, 1))
         for i in (1, 0):
-            quantise(h1_grouped[i], h1_codes[i], h1_scales[i])
+            quantise(h1_grouped[i][:], h1_codes[i][:], h1_scales[i][:])
         keep_h1(1, slice(1, PACK))
         for c in range(PACK):
             for i in (1, 0):

from contextlib import ExitStack

import concourse.mybir as mybir
from concourse.masks import make_identity

F32 = mybir.dt.float32
BF16 = mybir.dt.bfloat16
U32 = mybir.dt.uint32
U8 = mybir.dt.uint8
FP8X4 = mybir.dt.float8_e4m3fn_x4
MULT = mybir.AluOpType.mult
ADD = mybir.AluOpType.add

P = 128
PACK = 4
BATCH = 2
NODES = P * PACK
FEAT = 64
COLS = BATCH * FEAT
SUPPORTS = 2
HOPS = 2
RESULTS = SUPPORTS * HOPS
HALF = PACK // 2

FLOPS = 2 * RESULTS * NODES * NODES * COLS


def tile_ginconvfft_pa_s_kernel(tc, x, support, eps, out):
    nc = tc.nc
    with ExitStack() as ctx:
        keep = ctx.enter_context(tc.tile_pool(name="keep", bufs=1))
        psum = ctx.enter_context(tc.psum_pool(name="psum", bufs=1))
        ctx.enter_context(tc.manual_schedule())

        a_rows = {}
        x_rows = keep.tile([P, BATCH, PACK, FEAT], BF16)

        def load_support(i, first, end):
            rows = keep.tile([P, end - first, NODES], BF16, name="a_rows_%d_%d" % (i, first))
            by_half = support[i].rearrange("(u p e) m -> u p e m", u=2, e=HALF)[first // HALF]
            nc.sync.dma_start(out=rows[:], in_=by_half[:, first % HALF : first % HALF + end - first, :])
            for c in range(first, end):
                a_rows[i, c] = rows[:, c - first, :]

        load_support(0, 0, 2)
        for u in range(2):
            nc.sync.dma_start(
                out=x_rows[:, :, u * HALF : (u + 1) * HALF, :].rearrange("p b e f -> p b (e f)"),
                in_=x.rearrange("b (u p e) l h -> u p b (e l h)", u=2, e=HALF)[u],
            )
        load_support(0, 2, 4)
        load_support(1, 0, 1)
        load_support(1, 1, 2)
        load_support(1, 2, 3)
        load_support(1, 3, 4)

        identity = keep.tile([P, P], F32)
        make_identity(nc, identity[:])

        zero = keep.tile([P, 1], F32)
        nc.vector.memset(zero[:], 0.0)
        warm = psum.tile([P, NODES], F32, tag="spare")

        def load_tensor(n):
            nc.tensor.matmul(
                warm[:, :n],
                lhsT=zero[:].to_broadcast([P, P]),
                rhs=zero[:].to_broadcast([P, n]),
                start=True,
                stop=True,
            )

        load_tensor(NODES)
        eps_col = keep.tile([P, 2], BF16)
        nc.vector.memset(eps_col[:], 0.0)
        nc.scalar.dma_start(out=eps_col[0:1, 0:1], in_=eps.unsqueeze(0))
        ones = keep.tile([P, P], BF16)
        nc.vector.memset(ones[:], 1.0)
        eps_all = warm[:, :2]

        turned = {}
        a_grouped = {}
        a_codes = {}
        a_scales = {}

        def turn(i, c):
            words = a_rows[i, c].bitcast(F32)
            turned[i, c] = psum.tile([P, 2, P], F32, tag="bank", bufs=5, name="turned_%d_%d" % (i, c))
            for u in range(2):
                nc.tensor.transpose(turned[i, c][:, u, :], words[:, u * P : (u + 1) * P], identity[:])

        for i in range(SUPPORTS):
            for half in range(2):
                a_grouped[i, half] = keep.tile([P, HALF * P, PACK], BF16, align_bytes=64, name="a_grouped_%d_%d" % (i, half))
                a_codes[i, half] = keep.tile([P, HALF * P], U32, align_bytes=64, name="a_codes_%d_%d" % (i, half))
                a_scales[i, half] = keep.tile([P, HALF * P], U8, align_bytes=64, name="a_scales_%d_%d" % (i, half))

        def in_half(c):
            return slice((c % HALF) * P, (c % HALF + 1) * P)

        def group(i, c, copy=nc.scalar.copy):
            copy(
                out=a_grouped[i, c // HALF][:, in_half(c), :].bitcast(F32),
                in_=turned[i, c][:].rearrange("q u r -> q r u"),
            )

        def quantise(in_, codes, scales):
            nc.vector.quantize_mx(out=codes.bitcast(FP8X4), scales=scales, in_=in_.rearrange("p w t -> p (w t)"))

        def quantise_support(i, half, rows=slice(0, HALF * P)):
            quantise(a_grouped[i, half][:, rows, :], a_codes[i, half][:, rows], a_scales[i, half][:, rows])

        def multiply(sums, i, c, v):
            nc.tensor.matmul_mx(
                out=sums,
                lhsT=a_codes[i, c // HALF][:, in_half(c)].bitcast(FP8X4),
                lhsT_scale=a_scales[i, c // HALF][:, in_half(c)],
                rhs=v[0][:].bitcast(FP8X4),
                rhs_scale=v[1][:],
                start=True,
                stop=True,
            )

        def self_plus(out_, in0, in1):
            nc.vector.scalar_tensor_tensor(out=out_, in0=in0, scalar=gain[:], in1=in1, op0=MULT, op1=ADD)

        x_grouped = keep.tile([P, COLS, PACK], BF16, align_bytes=64)
        x_codes = keep.tile([P, COLS], U32, align_bytes=64)
        x_scales = keep.tile([P, COLS], U8, align_bytes=64)
        gain = keep.tile([P, 1], F32)
        base = keep.tile([P, RESULTS, PACK, COLS], F32)
        h1_grouped = {}
        h1_codes = {}
        h1_scales = {}
        sums1 = {}
        for i in range(SUPPORTS):
            h1_grouped[i] = keep.tile([P, COLS, PACK], BF16, align_bytes=64, name="h1_grouped_%d" % i)
            h1_codes[i] = keep.tile([P, COLS], U32, align_bytes=64, name="h1_codes_%d" % i)
            h1_scales[i] = keep.tile([P, COLS], U8, align_bytes=64, name="h1_scales_%d" % i)
            sums1[i] = psum.tile([P, PACK, COLS], F32, name="sums1_%d" % i)
        xv = (x_codes, x_scales)

        def keep_h1(i, classes, cols=slice(0, COLS)):
            self_plus(
                base[:, HOPS * i + 1, classes, cols],
                x_grouped[:, cols, classes].rearrange("p w c -> p c w"),
                sums1[i][:, classes, cols],
            )

        for c in range(PACK):
            turn(0, c)
            if c == 1:
                load_tensor(160)
        group(0, 0)
        nc.vector.tensor_copy(
            out=x_grouped[:].rearrange("p (b f) c -> p b f c", b=BATCH),
            in_=x_rows[:].rearrange("p b c f -> p b f c"),
        )
        group(0, 1)
        quantise(x_grouped[:], x_codes[:], x_scales[:])
        group(0, 2)
        quantise_support(0, 0)
        group(0, 3, nc.vector.tensor_copy)
        quantise_support(0, 1)
        for c in range(PACK):
            turn(1, c)
            if c == 1:
                load_tensor(P)
            group(1, c)
        nc.tensor.matmul(eps_all, lhsT=ones[:], rhs=eps_col[:], start=True, stop=True)
        for c in range(PACK):
            multiply(sums1[0][:, c, :], 0, c, xv)
        quantise_support(1, 0)
        nc.vector.tensor_scalar_add(out=gain[:], in0=eps_all[:, 0:1], scalar1=1.0)
        for c in (2, 3):
            quantise_support(1, 1, in_half(c))
        nc.scalar.copy(out=base[:, 0, :, :], in_=x_grouped[:].rearrange("p w c -> p c w"))
        for b in range(BATCH):
            cols = slice(b * FEAT, (b + 1) * FEAT)
            keep_h1(0, slice(0, PACK), cols)
            nc.scalar.copy(out=h1_grouped[0][:, cols, :], in_=base[:, 1, :, cols].rearrange("p c w -> p w c"))
        nc.scalar.copy(out=base[:, 2, :, :], in_=x_grouped[:].rearrange("p w c -> p c w"))
        sums = {}
        for c in range(PACK):
            sums[c] = psum.tile([P, RESULTS, COLS], F32, tag="bank", bufs=5, name="sums_%d" % c)
            multiply(sums[c][:, 0, :], 0, c, xv)
        for c in range(PACK):
            multiply(sums1[1][:, c, :], 1, c, xv)
        self_plus(h1_grouped[1][:], x_grouped[:], sums1[1][:].rearrange("p c w -> p w c"))
        for c in range(PACK):
            multiply(sums[c][:, 2, :], 1, c, xv)
        keep_h1(1, slice(0, 1))
        for i in (1, 0):
            quantise(h1_grouped[i][:], h1_codes[i][:], h1_scales[i][:])
        keep_h1(1, slice(1, PACK))
        for c in range(PACK):
            for i in (1, 0):
                multiply(sums[c][:, HOPS * i + 1, :], i, c, (h1_codes[i], h1_scales[i]))

        out_by_class = out.rearrange("b (u p e) l g -> u e p b (l g)", u=2, e=HALF)

        for c in range(PACK):
            woven = keep.tile([P, COLS, RESULTS], F32, name="woven_%d" % c)
            self_plus(
                woven[:],
                base[:, :, c, :].rearrange("p k w -> p w k"),
                sums[c][:].rearrange("p k w -> p w k"),
            )
            nc.sync.dma_start(
                out=out_by_class[c // HALF, c % HALF],
                in_=woven[:].rearrange("p (b f) k -> p b (f k)", b=BATCH),
            )
